import numpy as np
import ml_dtypes

BF16 = ml_dtypes.bfloat16


def bf(x):
    return np.asarray(x, np.float32).astype(BF16)


def f32(x):
    return np.asarray(x, np.float32)


def f64(x):
    return np.asarray(x).astype(np.float64)


def striped(idx):
    return np.tile(idx.reshape(-1, 16).T, (8, 1))


D, S, N, R, T = 128, 4096, 1024, 4, 256


def sigmoid(v):
    return 1.0 / (1.0 + np.exp(-v))


def setup_inputs():
    mu = 0.5 * np.random.standard_normal((D, 1))
    return {
        "table": bf(mu + np.random.standard_normal((D, S))),
        "w_word": bf(1.5 * np.random.standard_normal((D, D)) / np.sqrt(D)),
        "w_sent": bf(2.0 * np.random.standard_normal((D, D)) / np.sqrt(D)),
        "w_forget": bf(2.0 * np.random.standard_normal((D, D)) / np.sqrt(D)),
        "b_word": f32(np.random.standard_normal((D, 1))),
        "b_forget": f32(0.5 * np.random.standard_normal((D, 1))),
        "offs": striped(np.random.permutation(np.tile(np.arange(S), 2))[:N]),
    }


def reference(table, w_word, w_sent, w_forget, b_word, b_forget, offs):
    idx = offs[:16].T.reshape(-1)
    e = f64(table)[:, idx]
    p = (f64(w_word).T @ e).reshape(D, R, T)
    q = (f64(w_sent).T @ e).reshape(D, R, T).mean(axis=2, keepdims=True)
    a = (f64(w_forget).T @ e).reshape(D, R, T).mean(axis=2, keepdims=True)
    f = sigmoid(a + f64(b_forget)[:, :, None])
    x = np.exp(sigmoid(p + q + f64(b_word)[:, :, None]))
    share = x / x.mean(axis=2, keepdims=True)
    return (e.reshape(D, R, T) * (share + f)).reshape(D, N)

@@ -1,0 +1,102 @@
+import concourse.mybir as mybir
+from concourse.masks import make_identity
+
+D, S, N, R, T = 128, 4096, 1024, 4, 256
+PIECE = 512
+SENTENCES = PIECE // T
+FLOPS = 3 * 2 * D * D * N
+
+BF16, F32, U16 = mybir.dt.bfloat16, mybir.dt.float32, mybir.dt.uint16
+MULT, ADD = mybir.AluOpType.mult, mybir.AluOpType.add
+TANH, EXP = mybir.ActivationFunctionType.Tanh, mybir.ActivationFunctionType.Exp
+X_AXIS = mybir.AxisListType.X
+
+
+def tile_slstm_kernel(tc, table, w_word, w_sent, w_forget, b_word, b_forget, offs, out):
+    nc = tc.nc
+    with (
+        tc.tile_pool(name="held", bufs=1) as held,
+        tc.tile_pool(name="work", bufs=2) as work,
+        tc.psum_pool(name="psum", bufs=2) as psum,
+    ):
+        offsets = held.tile([D, N // 16], U16, name="offsets")
+        nc.sync.dma_start(offsets[:], offs)
+        words = held.tile([D, S], BF16, name="words")
+        nc.sync.dma_start(words[:], table)
+        sent_w = held.tile([D, D], BF16, name="sent_w")
+        nc.scalar.dma_start(sent_w[:], w_sent)
+        word_w = held.tile([D, D], BF16, name="word_w")
+        nc.scalar.dma_start(word_w[:], w_word)
+        forget_w = held.tile([D, D], BF16, name="forget_w")
+        nc.scalar.dma_start(forget_w[:], w_forget)
+        word_b = held.tile([D, 1], F32, name="word_b")
+        nc.gpsimd.dma_start(word_b[:], b_word)
+        forget_b = held.tile([D, 1], F32, name="forget_b")
+        nc.gpsimd.dma_start(forget_b[:], b_forget)
+        identity = held.tile([D, D], BF16, name="identity")
+        make_identity(nc, identity[:])
+
+        half_word_b = held.tile([D, 1], F32, name="half_word_b")
+        nc.vector.tensor_scalar(half_word_b[:], word_b[:], 0.5, None, op0=MULT)
+        half_forget_b = held.tile([D, 1], F32, name="half_forget_b")
+        nc.vector.tensor_scalar(half_forget_b[:], forget_b[:], 0.5, None, op0=MULT)
+
+        q_sum = held.tile([D, R], F32, name="q_sum")
+        a_sum = held.tile([D, R], F32, name="a_sum")
+        gate_bias = held.tile([D, R], F32, name="gate_bias")
+        f_tanh = held.tile([D, R], F32, name="f_tanh")
+        f_over_t = held.tile([D, R], F32, name="f_over_t")
+        x_sum = held.tile([D, R], F32, name="x_sum")
+        x_sum_inv = held.tile([D, R], F32, name="x_sum_inv")
+        result = held.tile([D, N], F32, name="result")
+
+        for h in range(N // PIECE):
+            piece_offsets = offsets[:, h * (PIECE // 16) : (h + 1) * (PIECE // 16)]
+            of_piece = slice(h * SENTENCES, (h + 1) * SENTENCES)
+
+            sent_proj = psum.tile([D, PIECE], F32, name="sent_proj")
+            nc.tensor.matmul(sent_proj[:], sent_w[:], words[:].indirect(piece_offsets), start=True, stop=True)
+            word_proj = psum.tile([D, PIECE], F32, name="word_proj")
+            nc.tensor.matmul(word_proj[:], word_w[:], words[:].indirect(piece_offsets), start=True, stop=True)
+            forget_proj = psum.tile([D, PIECE], F32, name="forget_proj")
+            nc.tensor.matmul(forget_proj[:], forget_w[:], words[:].indirect(piece_offsets), start=True, stop=True)
+            picked = psum.tile([D, PIECE], F32, name="picked")
+            nc.tensor.matmul(picked[:], identity[:], words[:].indirect(piece_offsets), start=True, stop=True)
+
+            nc.vector.reduce_sum(
+                q_sum[:, of_piece], sent_proj[:].rearrange("p (r t) -> p r t", t=T), axis=X_AXIS
+            )
+            nc.vector.tensor_scalar(
+                gate_bias[:, of_piece], q_sum[:, of_piece], 0.5 / T, half_word_b[:, 0:1], op0=MULT, op1=ADD
+            )
+            nc.vector.reduce_sum(
+                a_sum[:, of_piece], forget_proj[:].rearrange("p (r t) -> p r t", t=T), axis=X_AXIS
+            )
+            nc.scalar.activation(
+                f_tanh[:, of_piece], a_sum[:, of_piece], TANH, bias=half_forget_b[:, 0:1], scale=0.5 / T
+            )
+            nc.vector.tensor_scalar(
+                f_over_t[:, of_piece], f_tanh[:, of_piece], 0.5 / T, 0.5 / T, op0=MULT, op1=ADD
+            )
+
+            for s in range(SENTENCES):
+                r = h * SENTENCES + s
+                in_piece = slice(s * T, (s + 1) * T)
+                gate = work.tile([D, T], F32, name="gate")
+                nc.scalar.activation(
+                    gate[:], word_proj[:, in_piece], TANH, bias=gate_bias[:, r : r + 1], scale=0.5
+                )
+                x = work.tile([D, T], F32, name="x")
+                nc.scalar.activation(x[:], gate[:], EXP, scale=0.5, accum_out=x_sum[:, r : r + 1])
+                nc.vector.reciprocal(x_sum_inv[:, r : r + 1], x_sum[:, r : r + 1])
+                weight = work.tile([D, T], F32, name="weight")
+                nc.vector.tensor_scalar(
+                    weight[:], x[:], x_sum_inv[:, r : r + 1], f_over_t[:, r : r + 1], op0=MULT, op1=ADD
+                )
+                nc.vector.scalar_tensor_tensor(
+                    result[:, r * T : (r + 1) * T], weight[:], float(T), picked[:, in_piece], op0=MULT, op1=MULT
+                )
+
+            nc.sync.dma_start(
+                out[:, h * PIECE : (h + 1) * PIECE], result[:, h * PIECE : (h + 1) * PIECE]
+            )

@@ -3,6 +3,7 @@ from concourse.masks import make_identity
 
 D, S, N, R, T = 128, 4096, 1024, 4, 256
 PIECE = 512
+PIECES = N // PIECE
 SENTENCES = PIECE // T
 FLOPS = 3 * 2 * D * D * N
 
@@ -17,7 +18,7 @@ def tile_slstm_kernel(tc, table, w_word, w_sent, w_forget, b_word, b_forget, off
     with (
         tc.tile_pool(name="held", bufs=1) as held,
         tc.tile_pool(name="work", bufs=2) as work,
-        tc.psum_pool(name="psum", bufs=2) as psum,
+        tc.psum_pool(name="psum", bufs=1) as psum,
     ):
         offsets = held.tile([D, N // 16], U16, name="offsets")
         nc.sync.dma_start(offsets[:], offs)
@@ -45,58 +46,61 @@ def tile_slstm_kernel(tc, table, w_word, w_sent, w_forget, b_word, b_forget, off
         a_sum = held.tile([D, R], F32, name="a_sum")
         gate_bias = held.tile([D, R], F32, name="gate_bias")
         f_tanh = held.tile([D, R], F32, name="f_tanh")
-        f_over_t = held.tile([D, R], F32, name="f_over_t")
+        f = held.tile([D, R], F32, name="f")
         x_sum = held.tile([D, R], F32, name="x_sum")
         x_sum_inv = held.tile([D, R], F32, name="x_sum_inv")
         result = held.tile([D, N], F32, name="result")
 
-        for h in range(N // PIECE):
-            piece_offsets = offsets[:, h * (PIECE // 16) : (h + 1) * (PIECE // 16)]
+        def looked_up(h):
+            return words[:].indirect(offsets[:, h * (PIECE // 16) : (h + 1) * (PIECE // 16)])
+
+        def by_sentence(product):
+            return product[:].rearrange("p (r t) -> p r t", t=T)
+
+        sent_proj = [psum.tile([D, PIECE], F32, name=f"sent_proj{h}") for h in range(PIECES)]
+        word_proj = [psum.tile([D, PIECE], F32, name=f"word_proj{h}") for h in range(PIECES)]
+        forget_proj = [psum.tile([D, PIECE], F32, name=f"forget_proj{h}") for h in range(PIECES)]
+        picked = [psum.tile([D, PIECE], F32, name=f"picked{h}") for h in range(PIECES)]
+        for h in range(PIECES):
+            nc.tensor.matmul(sent_proj[h][:], sent_w[:], looked_up(h), start=True, stop=True)
+            nc.tensor.matmul(word_proj[h][:], word_w[:], looked_up(h), start=True, stop=True)
+        for h in range(PIECES):
+            nc.tensor.matmul(forget_proj[h][:], forget_w[:], looked_up(h), start=True, stop=True)
+        for h in range(PIECES):
+            nc.tensor.matmul(picked[h][:], identity[:], looked_up(h), start=True, stop=True)
+
+        for h in range(PIECES):
             of_piece = slice(h * SENTENCES, (h + 1) * SENTENCES)
-
-            sent_proj = psum.tile([D, PIECE], F32, name="sent_proj")
-            nc.tensor.matmul(sent_proj[:], sent_w[:], words[:].indirect(piece_offsets), start=True, stop=True)
-            word_proj = psum.tile([D, PIECE], F32, name="word_proj")
-            nc.tensor.matmul(word_proj[:], word_w[:], words[:].indirect(piece_offsets), start=True, stop=True)
-            forget_proj = psum.tile([D, PIECE], F32, name="forget_proj")
-            nc.tensor.matmul(forget_proj[:], forget_w[:], words[:].indirect(piece_offsets), start=True, stop=True)
-            picked = psum.tile([D, PIECE], F32, name="picked")
-            nc.tensor.matmul(picked[:], identity[:], words[:].indirect(piece_offsets), start=True, stop=True)
-
-            nc.vector.reduce_sum(
-                q_sum[:, of_piece], sent_proj[:].rearrange("p (r t) -> p r t", t=T), axis=X_AXIS
-            )
+            nc.vector.reduce_sum(q_sum[:, of_piece], by_sentence(sent_proj[h]), axis=X_AXIS)
             nc.vector.tensor_scalar(
                 gate_bias[:, of_piece], q_sum[:, of_piece], 0.5 / T, half_word_b[:, 0:1], op0=MULT, op1=ADD
             )
-            nc.vector.reduce_sum(
-                a_sum[:, of_piece], forget_proj[:].rearrange("p (r t) -> p r t", t=T), axis=X_AXIS
-            )
-            nc.scalar.activation(
-                f_tanh[:, of_piece], a_sum[:, of_piece], TANH, bias=half_forget_b[:, 0:1], scale=0.5 / T
-            )
-            nc.vector.tensor_scalar(
-                f_over_t[:, of_piece], f_tanh[:, of_piece], 0.5 / T, 0.5 / T, op0=MULT, op1=ADD
-            )
 
+        shares = []
+        for h in range(PIECES):
             for s in range(SENTENCES):
                 r = h * SENTENCES + s
-                in_piece = slice(s * T, (s + 1) * T)
                 gate = work.tile([D, T], F32, name="gate")
                 nc.scalar.activation(
-                    gate[:], word_proj[:, in_piece], TANH, bias=gate_bias[:, r : r + 1], scale=0.5
+                    gate[:], word_proj[h][:, s * T : (s + 1) * T], TANH, bias=gate_bias[:, r : r + 1], scale=0.5
                 )
                 x = work.tile([D, T], F32, name="x")
                 nc.scalar.activation(x[:], gate[:], EXP, scale=0.5, accum_out=x_sum[:, r : r + 1])
                 nc.vector.reciprocal(x_sum_inv[:, r : r + 1], x_sum[:, r : r + 1])
-                weight = work.tile([D, T], F32, name="weight")
-                nc.vector.tensor_scalar(
-                    weight[:], x[:], x_sum_inv[:, r : r + 1], f_over_t[:, r : r + 1], op0=MULT, op1=ADD
-                )
-                nc.vector.scalar_tensor_tensor(
-                    result[:, r * T : (r + 1) * T], weight[:], float(T), picked[:, in_piece], op0=MULT, op1=MULT
-                )
+                share = held.tile([D, T], F32, name=f"share{r}")
+                nc.vector.tensor_scalar(share[:], x[:], x_sum_inv[:, r : r + 1], float(T), op0=MULT, op1=MULT)
+                shares.append(share)
+            of_piece = slice(h * SENTENCES, (h + 1) * SENTENCES)
+            nc.vector.reduce_sum(a_sum[:, of_piece], by_sentence(forget_proj[h]), axis=X_AXIS)
 
-            nc.sync.dma_start(
-                out[:, h * PIECE : (h + 1) * PIECE], result[:, h * PIECE : (h + 1) * PIECE]
+        nc.scalar.activation(f_tanh[:], a_sum[:], TANH, bias=half_forget_b[:, 0:1], scale=0.5 / T)
+        nc.vector.tensor_scalar(f[:], f_tanh[:], 0.5, 0.5, op0=MULT, op1=ADD)
+
+        for r in range(R):
+            h, s = divmod(r, SENTENCES)
+            of_sentence = slice(r * T, (r + 1) * T)
+            nc.vector.scalar_tensor_tensor(
+                result[:, of_sentence], shares[r][:], f[:, r : r + 1], picked[h][:, s * T : (s + 1) * T],
+                op0=ADD, op1=MULT,
             )
+            nc.sync.dma_start(out[:, of_sentence], result[:, of_sentence])

@@ -6,6 +6,7 @@ PIECE = 512
 PIECES = N // PIECE
 SENTENCES = PIECE // T
 FLOPS = 3 * 2 * D * D * N
+WARM_UPS = 8
 
 BF16, F32, U16 = mybir.dt.bfloat16, mybir.dt.float32, mybir.dt.uint16
 MULT, ADD = mybir.AluOpType.mult, mybir.AluOpType.add
@@ -26,81 +27,86 @@ def tile_slstm_kernel(tc, table, w_word, w_sent, w_forget, b_word, b_forget, off
         nc.sync.dma_start(words[:], table)
         sent_w = held.tile([D, D], BF16, name="sent_w")
         nc.scalar.dma_start(sent_w[:], w_sent)
+        word_b = held.tile([D, 1], F32, name="word_b")
+        nc.scalar.dma_start(word_b[:], b_word)
         word_w = held.tile([D, D], BF16, name="word_w")
         nc.scalar.dma_start(word_w[:], w_word)
         forget_w = held.tile([D, D], BF16, name="forget_w")
-        nc.scalar.dma_start(forget_w[:], w_forget)
-        word_b = held.tile([D, 1], F32, name="word_b")
-        nc.gpsimd.dma_start(word_b[:], b_word)
+        nc.gpsimd.dma_start(forget_w[:], w_forget)
         forget_b = held.tile([D, 1], F32, name="forget_b")
         nc.gpsimd.dma_start(forget_b[:], b_forget)
         identity = held.tile([D, D], BF16, name="identity")
         make_identity(nc, identity[:])
 
+        sent_proj = [psum.tile([D, PIECE], F32, name=f"sent_proj{h}") for h in range(PIECES)]
+        word_proj = [psum.tile([D, PIECE], F32, name=f"word_proj{h}") for h in range(PIECES)]
+        forget_proj = [psum.tile([D, PIECE], F32, name=f"forget_proj{h}") for h in range(PIECES)]
+        picked = [psum.tile([D, PIECE], F32, name=f"picked{h}") for h in range(PIECES)]
+
+        zeros = held.tile([D, PIECE], BF16, name="zeros")
+        nc.vector.memset(zeros[:], 0.0)
+        for i in range(WARM_UPS):
+            nc.tensor.matmul(picked[PIECES - 1][:], zeros[:, :D], zeros[:], start=True, stop=True)
+        table_loaded = held.tile([D, 1], F32, name="table_loaded")
+        nc.scalar.activation(table_loaded[:], zeros[:, 0:1], TANH)
+
+        HALF_MEAN = 0.5 / T
         half_word_b = held.tile([D, 1], F32, name="half_word_b")
         nc.vector.tensor_scalar(half_word_b[:], word_b[:], 0.5, None, op0=MULT)
         half_forget_b = held.tile([D, 1], F32, name="half_forget_b")
         nc.vector.tensor_scalar(half_forget_b[:], forget_b[:], 0.5, None, op0=MULT)
 
-        q_sum = held.tile([D, R], F32, name="q_sum")
-        a_sum = held.tile([D, R], F32, name="a_sum")
-        gate_bias = held.tile([D, R], F32, name="gate_bias")
-        f_tanh = held.tile([D, R], F32, name="f_tanh")
-        f = held.tile([D, R], F32, name="f")
-        x_sum = held.tile([D, R], F32, name="x_sum")
-        x_sum_inv = held.tile([D, R], F32, name="x_sum_inv")
-        result = held.tile([D, N], F32, name="result")
-
         def looked_up(h):
             return words[:].indirect(offsets[:, h * (PIECE // 16) : (h + 1) * (PIECE // 16)])
 
-        def by_sentence(product):
-            return product[:].rearrange("p (r t) -> p r t", t=T)
-
-        sent_proj = [psum.tile([D, PIECE], F32, name=f"sent_proj{h}") for h in range(PIECES)]
-        word_proj = [psum.tile([D, PIECE], F32, name=f"word_proj{h}") for h in range(PIECES)]
-        forget_proj = [psum.tile([D, PIECE], F32, name=f"forget_proj{h}") for h in range(PIECES)]
-        picked = [psum.tile([D, PIECE], F32, name=f"picked{h}") for h in range(PIECES)]
-        for h in range(PIECES):
-            nc.tensor.matmul(sent_proj[h][:], sent_w[:], looked_up(h), start=True, stop=True)
-            nc.tensor.matmul(word_proj[h][:], word_w[:], looked_up(h), start=True, stop=True)
-        for h in range(PIECES):
-            nc.tensor.matmul(forget_proj[h][:], forget_w[:], looked_up(h), start=True, stop=True)
+        nc.tensor.matmul(sent_proj[0][:], sent_w[:], looked_up(0), start=True, stop=True)
+        nc.tensor.matmul(word_proj[0][:], word_w[:], looked_up(0), start=True, stop=True)
+        nc.tensor.matmul(sent_proj[1][:], sent_w[:], looked_up(1), start=True, stop=True)
+        nc.tensor.matmul(forget_proj[0][:], forget_w[:], looked_up(0), start=True, stop=True)
+        nc.tensor.matmul(word_proj[1][:], word_w[:], looked_up(1), start=True, stop=True)
+        nc.tensor.matmul(forget_proj[1][:], forget_w[:], looked_up(1), start=True, stop=True)
         for h in range(PIECES):
             nc.tensor.matmul(picked[h][:], identity[:], looked_up(h), start=True, stop=True)
 
-        for h in range(PIECES):
-            of_piece = slice(h * SENTENCES, (h + 1) * SENTENCES)
-            nc.vector.reduce_sum(q_sum[:, of_piece], by_sentence(sent_proj[h]), axis=X_AXIS)
-            nc.vector.tensor_scalar(
-                gate_bias[:, of_piece], q_sum[:, of_piece], 0.5 / T, half_word_b[:, 0:1], op0=MULT, op1=ADD
-            )
-
-        shares = []
-        for h in range(PIECES):
-            for s in range(SENTENCES):
-                r = h * SENTENCES + s
-                gate = work.tile([D, T], F32, name="gate")
-                nc.scalar.activation(
-                    gate[:], word_proj[h][:, s * T : (s + 1) * T], TANH, bias=gate_bias[:, r : r + 1], scale=0.5
-                )
-                x = work.tile([D, T], F32, name="x")
-                nc.scalar.activation(x[:], gate[:], EXP, scale=0.5, accum_out=x_sum[:, r : r + 1])
-                nc.vector.reciprocal(x_sum_inv[:, r : r + 1], x_sum[:, r : r + 1])
-                share = held.tile([D, T], F32, name=f"share{r}")
-                nc.vector.tensor_scalar(share[:], x[:], x_sum_inv[:, r : r + 1], float(T), op0=MULT, op1=MULT)
-                shares.append(share)
-            of_piece = slice(h * SENTENCES, (h + 1) * SENTENCES)
-            nc.vector.reduce_sum(a_sum[:, of_piece], by_sentence(forget_proj[h]), axis=X_AXIS)
-
-        nc.scalar.activation(f_tanh[:], a_sum[:], TANH, bias=half_forget_b[:, 0:1], scale=0.5 / T)
-        nc.vector.tensor_scalar(f[:], f_tanh[:], 0.5, 0.5, op0=MULT, op1=ADD)
-
+        gate_bias = [held.tile([D, 1], F32, name=f"gate_bias{r}") for r in range(R)]
         for r in range(R):
             h, s = divmod(r, SENTENCES)
-            of_sentence = slice(r * T, (r + 1) * T)
-            nc.vector.scalar_tensor_tensor(
-                result[:, of_sentence], shares[r][:], f[:, r : r + 1], picked[h][:, s * T : (s + 1) * T],
-                op0=ADD, op1=MULT,
+            unused = work.tile([D, T], F32, name="unused")
+            nc.vector.tensor_scalar(
+                unused[:], sent_proj[h][:, s * T : (s + 1) * T], HALF_MEAN, half_word_b[:],
+                op0=MULT, op1=ADD, accum_out=gate_bias[r][:],
             )
-            nc.sync.dma_start(out[:, of_sentence], result[:, of_sentence])
+
+        result = held.tile([D, N], F32, name="result")
+        for h in range(PIECES):
+            sentences = range(h * SENTENCES, (h + 1) * SENTENCES)
+
+            a_sum = held.tile([D, SENTENCES], F32, name=f"a_sum{h}")
+            nc.vector.reduce_sum(a_sum[:], forget_proj[h][:].rearrange("p (r t) -> p r t", t=T), axis=X_AXIS)
+            f_tanh = held.tile([D, SENTENCES], F32, name=f"f_tanh{h}")
+            nc.scalar.activation(f_tanh[:], a_sum[:], TANH, bias=half_forget_b[:], scale=HALF_MEAN)
+            f = held.tile([D, SENTENCES], F32, name=f"f{h}")
+            nc.vector.tensor_scalar(f[:], f_tanh[:], 0.5, 0.5, op0=MULT, op1=ADD)
+
+            gate = {r: held.tile([D, T], F32, name=f"gate{r}") for r in sentences}
+            x = {r: held.tile([D, T], F32, name=f"x{r}") for r in sentences}
+            x_sum = {r: held.tile([D, 1], F32, name=f"x_sum{r}") for r in sentences}
+            x_sum_inv = {r: held.tile([D, 1], F32, name=f"x_sum_inv{r}") for r in sentences}
+            share = {r: held.tile([D, T], F32, name=f"share{r}") for r in sentences}
+            for r in sentences:
+                in_piece = slice((r - h * SENTENCES) * T, (r - h * SENTENCES + 1) * T)
+                nc.scalar.activation(gate[r][:], word_proj[h][:, in_piece], TANH, bias=gate_bias[r][:], scale=0.5)
+            for r in sentences:
+                nc.scalar.activation(x[r][:], gate[r][:], EXP, scale=0.5, accum_out=x_sum[r][:])
+            for r in sentences:
+                nc.vector.reciprocal(x_sum_inv[r][:], x_sum[r][:])
+                nc.vector.tensor_scalar(share[r][:], x[r][:], x_sum_inv[r][:], float(T), op0=MULT, op1=MULT)
+
+            for r in sentences:
+                s = r - h * SENTENCES
+                of_sentence = slice(r * T, (r + 1) * T)
+                nc.vector.scalar_tensor_tensor(
+                    result[:, of_sentence], share[r][:], f[:, s : s + 1], picked[h][:, s * T : (s + 1) * T],
+                    op0=ADD, op1=MULT,
+                )
+                nc.sync.dma_start(out[:, of_sentence], result[:, of_sentence])

@@ -6,7 +6,6 @@ PIECE = 512
 PIECES = N // PIECE
 SENTENCES = PIECE // T
 FLOPS = 3 * 2 * D * D * N
-WARM_UPS = 8
 
 BF16, F32, U16 = mybir.dt.bfloat16, mybir.dt.float32, mybir.dt.uint16
 MULT, ADD = mybir.AluOpType.mult, mybir.AluOpType.add
@@ -21,10 +20,10 @@ def tile_slstm_kernel(tc, table, w_word, w_sent, w_forget, b_word, b_forget, off
         tc.tile_pool(name="work", bufs=2) as work,
         tc.psum_pool(name="psum", bufs=1) as psum,
     ):
-        offsets = held.tile([D, N // 16], U16, name="offsets")
-        nc.sync.dma_start(offsets[:], offs)
         words = held.tile([D, S], BF16, name="words")
         nc.sync.dma_start(words[:], table)
+        offsets = held.tile([D, N // 16], U16, name="offsets")
+        nc.sync.dma_start(offsets[:], offs)
         sent_w = held.tile([D, D], BF16, name="sent_w")
         nc.scalar.dma_start(sent_w[:], w_sent)
         word_b = held.tile([D, 1], F32, name="word_b")
@@ -32,9 +31,9 @@ def tile_slstm_kernel(tc, table, w_word, w_sent, w_forget, b_word, b_forget, off
         word_w = held.tile([D, D], BF16, name="word_w")
         nc.scalar.dma_start(word_w[:], w_word)
         forget_w = held.tile([D, D], BF16, name="forget_w")
-        nc.gpsimd.dma_start(forget_w[:], w_forget)
+        nc.sync.dma_start(forget_w[:], w_forget)
         forget_b = held.tile([D, 1], F32, name="forget_b")
-        nc.gpsimd.dma_start(forget_b[:], b_forget)
+        nc.sync.dma_start(forget_b[:], b_forget)
         identity = held.tile([D, D], BF16, name="identity")
         make_identity(nc, identity[:])
 
@@ -43,12 +42,10 @@ def tile_slstm_kernel(tc, table, w_word, w_sent, w_forget, b_word, b_forget, off
         forget_proj = [psum.tile([D, PIECE], F32, name=f"forget_proj{h}") for h in range(PIECES)]
         picked = [psum.tile([D, PIECE], F32, name=f"picked{h}") for h in range(PIECES)]
 
-        zeros = held.tile([D, PIECE], BF16, name="zeros")
-        nc.vector.memset(zeros[:], 0.0)
-        for i in range(WARM_UPS):
-            nc.tensor.matmul(picked[PIECES - 1][:], zeros[:, :D], zeros[:], start=True, stop=True)
+        zero = held.tile([D, 1], F32, name="zero")
+        nc.vector.memset(zero[:], 0.0)
         table_loaded = held.tile([D, 1], F32, name="table_loaded")
-        nc.scalar.activation(table_loaded[:], zeros[:, 0:1], TANH)
+        nc.scalar.activation(table_loaded[:], zero[:], TANH)
 
         HALF_MEAN = 0.5 / T
         half_word_b = held.tile([D, 1], F32, name="half_word_b")

@@ -6,6 +6,7 @@ PIECE = 512
 PIECES = N // PIECE
 SENTENCES = PIECE // T
 FLOPS = 3 * 2 * D * D * N
+WARM_UPS = 4
 
 BF16, F32, U16 = mybir.dt.bfloat16, mybir.dt.float32, mybir.dt.uint16
 MULT, ADD = mybir.AluOpType.mult, mybir.AluOpType.add
@@ -42,10 +43,12 @@ def tile_slstm_kernel(tc, table, w_word, w_sent, w_forget, b_word, b_forget, off
         forget_proj = [psum.tile([D, PIECE], F32, name=f"forget_proj{h}") for h in range(PIECES)]
         picked = [psum.tile([D, PIECE], F32, name=f"picked{h}") for h in range(PIECES)]
 
-        zero = held.tile([D, 1], F32, name="zero")
-        nc.vector.memset(zero[:], 0.0)
+        zeros = held.tile([D, PIECE], BF16, name="zeros")
+        nc.vector.memset(zeros[:], 0.0)
+        for i in range(WARM_UPS):
+            nc.tensor.matmul(picked[PIECES - 1][:], zeros[:, :D], zeros[:], start=True, stop=True)
         table_loaded = held.tile([D, 1], F32, name="table_loaded")
-        nc.scalar.activation(table_loaded[:], zero[:], TANH)
+        nc.scalar.activation(table_loaded[:], zeros[:, 0:1], TANH)
 
         HALF_MEAN = 0.5 / T
         half_word_b = held.tile([D, 1], F32, name="half_word_b")

@@ -1,12 +1,16 @@
 import concourse.mybir as mybir
 from concourse.masks import make_identity
 
-D, S, N, R, T = 128, 4096, 1024, 4, 256
+D = 128
+S = 4096
+N = 1024
+T = 256
+R = N // T
 PIECE = 512
 PIECES = N // PIECE
-SENTENCES = PIECE // T
+PER_PIECE = PIECE // T
+HALF_MEAN = 0.5 / T
 FLOPS = 3 * 2 * D * D * N
-WARM_UPS = 4
 
 BF16, F32, U16 = mybir.dt.bfloat16, mybir.dt.float32, mybir.dt.uint16
 MULT, ADD = mybir.AluOpType.mult, mybir.AluOpType.add
@@ -18,7 +22,7 @@ def tile_slstm_kernel(tc, table, w_word, w_sent, w_forget, b_word, b_forget, off
     nc = tc.nc
     with (
         tc.tile_pool(name="held", bufs=1) as held,
-        tc.tile_pool(name="work", bufs=2) as work,
+        tc.tile_pool(name="scratch", bufs=2) as scratch,
         tc.psum_pool(name="psum", bufs=1) as psum,
     ):
         words = held.tile([D, S], BF16, name="words")
@@ -38,19 +42,11 @@ def tile_slstm_kernel(tc, table, w_word, w_sent, w_forget, b_word, b_forget, off
         identity = held.tile([D, D], BF16, name="identity")
         make_identity(nc, identity[:])
 
-        sent_proj = [psum.tile([D, PIECE], F32, name=f"sent_proj{h}") for h in range(PIECES)]
-        word_proj = [psum.tile([D, PIECE], F32, name=f"word_proj{h}") for h in range(PIECES)]
-        forget_proj = [psum.tile([D, PIECE], F32, name=f"forget_proj{h}") for h in range(PIECES)]
-        picked = [psum.tile([D, PIECE], F32, name=f"picked{h}") for h in range(PIECES)]
+        primer = held.tile([D, 1], F32, name="primer")
+        nc.vector.memset(primer[:], 0.0)
+        primed = held.tile([D, 1], F32, name="primed")
+        nc.scalar.activation(primed[:], primer[:], TANH)
 
-        zeros = held.tile([D, PIECE], BF16, name="zeros")
-        nc.vector.memset(zeros[:], 0.0)
-        for i in range(WARM_UPS):
-            nc.tensor.matmul(picked[PIECES - 1][:], zeros[:, :D], zeros[:], start=True, stop=True)
-        table_loaded = held.tile([D, 1], F32, name="table_loaded")
-        nc.scalar.activation(table_loaded[:], zeros[:, 0:1], TANH)
-
-        HALF_MEAN = 0.5 / T
         half_word_b = held.tile([D, 1], F32, name="half_word_b")
         nc.vector.tensor_scalar(half_word_b[:], word_b[:], 0.5, None, op0=MULT)
         half_forget_b = held.tile([D, 1], F32, name="half_forget_b")
@@ -59,54 +55,57 @@ def tile_slstm_kernel(tc, table, w_word, w_sent, w_forget, b_word, b_forget, off
         def looked_up(h):
             return words[:].indirect(offsets[:, h * (PIECE // 16) : (h + 1) * (PIECE // 16)])
 
-        nc.tensor.matmul(sent_proj[0][:], sent_w[:], looked_up(0), start=True, stop=True)
-        nc.tensor.matmul(word_proj[0][:], word_w[:], looked_up(0), start=True, stop=True)
-        nc.tensor.matmul(sent_proj[1][:], sent_w[:], looked_up(1), start=True, stop=True)
-        nc.tensor.matmul(forget_proj[0][:], forget_w[:], looked_up(0), start=True, stop=True)
-        nc.tensor.matmul(word_proj[1][:], word_w[:], looked_up(1), start=True, stop=True)
-        nc.tensor.matmul(forget_proj[1][:], forget_w[:], looked_up(1), start=True, stop=True)
+        sent_proj = [psum.tile([D, PIECE], F32, name=f"sent_proj{h}") for h in range(PIECES)]
+        word_proj = [psum.tile([D, PIECE], F32, name=f"word_proj{h}") for h in range(PIECES)]
+        forget_proj = [psum.tile([D, PIECE], F32, name=f"forget_proj{h}") for h in range(PIECES)]
+        picked = [psum.tile([D, PIECE], F32, name=f"picked{h}") for h in range(PIECES)]
+        for h in range(PIECES):
+            nc.tensor.matmul(sent_proj[h][:], sent_w[:], looked_up(h), start=True, stop=True)
+            nc.tensor.matmul(word_proj[h][:], word_w[:], looked_up(h), start=True, stop=True)
+        for h in range(PIECES):
+            nc.tensor.matmul(forget_proj[h][:], forget_w[:], looked_up(h), start=True, stop=True)
         for h in range(PIECES):
             nc.tensor.matmul(picked[h][:], identity[:], looked_up(h), start=True, stop=True)
 
+        def of_sentence(products, r):
+            h, s = divmod(r, PER_PIECE)
+            return products[h][:, s * T : (s + 1) * T]
+
         gate_bias = [held.tile([D, 1], F32, name=f"gate_bias{r}") for r in range(R)]
         for r in range(R):
-            h, s = divmod(r, SENTENCES)
-            unused = work.tile([D, T], F32, name="unused")
+            scaled = scratch.tile([D, T], F32, name="scaled")
             nc.vector.tensor_scalar(
-                unused[:], sent_proj[h][:, s * T : (s + 1) * T], HALF_MEAN, half_word_b[:],
+                scaled[:], of_sentence(sent_proj, r), HALF_MEAN, half_word_b[:],
                 op0=MULT, op1=ADD, accum_out=gate_bias[r][:],
             )
 
-        result = held.tile([D, N], F32, name="result")
+        gate = [held.tile([D, T], F32, name=f"gate{r}") for r in range(R)]
+        x = [held.tile([D, T], F32, name=f"x{r}") for r in range(R)]
+        x_sum = [held.tile([D, 1], F32, name=f"x_sum{r}") for r in range(R)]
+        x_sum_inv = [held.tile([D, 1], F32, name=f"x_sum_inv{r}") for r in range(R)]
+        share = [held.tile([D, T], F32, name=f"share{r}") for r in range(R)]
+        f = [held.tile([D, PER_PIECE], F32, name=f"f{h}") for h in range(PIECES)]
         for h in range(PIECES):
-            sentences = range(h * SENTENCES, (h + 1) * SENTENCES)
-
-            a_sum = held.tile([D, SENTENCES], F32, name=f"a_sum{h}")
+            a_sum = held.tile([D, PER_PIECE], F32, name=f"a_sum{h}")
             nc.vector.reduce_sum(a_sum[:], forget_proj[h][:].rearrange("p (r t) -> p r t", t=T), axis=X_AXIS)
-            f_tanh = held.tile([D, SENTENCES], F32, name=f"f_tanh{h}")
+            f_tanh = held.tile([D, PER_PIECE], F32, name=f"f_tanh{h}")
             nc.scalar.activation(f_tanh[:], a_sum[:], TANH, bias=half_forget_b[:], scale=HALF_MEAN)
-            f = held.tile([D, SENTENCES], F32, name=f"f{h}")
-            nc.vector.tensor_scalar(f[:], f_tanh[:], 0.5, 0.5, op0=MULT, op1=ADD)
+            nc.vector.tensor_scalar(f[h][:], f_tanh[:], 0.5, 0.5, op0=MULT, op1=ADD)
 
-            gate = {r: held.tile([D, T], F32, name=f"gate{r}") for r in sentences}
-            x = {r: held.tile([D, T], F32, name=f"x{r}") for r in sentences}
-            x_sum = {r: held.tile([D, 1], F32, name=f"x_sum{r}") for r in sentences}
-            x_sum_inv = {r: held.tile([D, 1], F32, name=f"x_sum_inv{r}") for r in sentences}
-            share = {r: held.tile([D, T], F32, name=f"share{r}") for r in sentences}
+            sentences = range(h * PER_PIECE, (h + 1) * PER_PIECE)
             for r in sentences:
-                in_piece = slice((r - h * SENTENCES) * T, (r - h * SENTENCES + 1) * T)
-                nc.scalar.activation(gate[r][:], word_proj[h][:, in_piece], TANH, bias=gate_bias[r][:], scale=0.5)
+                nc.scalar.activation(gate[r][:], of_sentence(word_proj, r), TANH, bias=gate_bias[r][:], scale=0.5)
             for r in sentences:
                 nc.scalar.activation(x[r][:], gate[r][:], EXP, scale=0.5, accum_out=x_sum[r][:])
             for r in sentences:
                 nc.vector.reciprocal(x_sum_inv[r][:], x_sum[r][:])
                 nc.vector.tensor_scalar(share[r][:], x[r][:], x_sum_inv[r][:], float(T), op0=MULT, op1=MULT)
 
-            for r in sentences:
-                s = r - h * SENTENCES
-                of_sentence = slice(r * T, (r + 1) * T)
-                nc.vector.scalar_tensor_tensor(
-                    result[:, of_sentence], share[r][:], f[:, s : s + 1], picked[h][:, s * T : (s + 1) * T],
-                    op0=ADD, op1=MULT,
-                )
-                nc.sync.dma_start(out[:, of_sentence], result[:, of_sentence])
+        result = held.tile([D, N], F32, name="result")
+        for r in range(R):
+            h, s = divmod(r, PER_PIECE)
+            nc.vector.scalar_tensor_tensor(
+                result[:, r * T : (r + 1) * T], share[r][:], f[h][:, s : s + 1], of_sentence(picked, r),
+                op0=ADD, op1=MULT,
+            )
+            nc.sync.dma_start(out[:, r * T : (r + 1) * T], result[:, r * T : (r + 1) * T])

@@ -6,9 +6,8 @@ S = 4096
 N = 1024
 T = 256
 R = N // T
-PIECE = 512
-PIECES = N // PIECE
-PER_PIECE = PIECE // T
+PAIR = 2
+PAIRS = R // PAIR
 HALF_MEAN = 0.5 / T
 FLOPS = 3 * 2 * D * D * N
 
@@ -23,7 +22,7 @@ def tile_slstm_kernel(tc, table, w_word, w_sent, w_forget, b_word, b_forget, off
     with (
         tc.tile_pool(name="held", bufs=1) as held,
         tc.tile_pool(name="scratch", bufs=2) as scratch,
-        tc.psum_pool(name="psum", bufs=1) as psum,
+        tc.psum_pool(name="psum", bufs=2) as psum,
     ):
         words = held.tile([D, S], BF16, name="words")
         nc.sync.dma_start(words[:], table)
@@ -52,60 +51,55 @@ def tile_slstm_kernel(tc, table, w_word, w_sent, w_forget, b_word, b_forget, off
         half_forget_b = held.tile([D, 1], F32, name="half_forget_b")
         nc.vector.tensor_scalar(half_forget_b[:], forget_b[:], 0.5, None, op0=MULT)
 
-        def looked_up(h):
-            return words[:].indirect(offsets[:, h * (PIECE // 16) : (h + 1) * (PIECE // 16)])
-
-        sent_proj = [psum.tile([D, PIECE], F32, name=f"sent_proj{h}") for h in range(PIECES)]
-        word_proj = [psum.tile([D, PIECE], F32, name=f"word_proj{h}") for h in range(PIECES)]
-        forget_proj = [psum.tile([D, PIECE], F32, name=f"forget_proj{h}") for h in range(PIECES)]
-        picked = [psum.tile([D, PIECE], F32, name=f"picked{h}") for h in range(PIECES)]
-        for h in range(PIECES):
-            nc.tensor.matmul(sent_proj[h][:], sent_w[:], looked_up(h), start=True, stop=True)
-            nc.tensor.matmul(word_proj[h][:], word_w[:], looked_up(h), start=True, stop=True)
-        for h in range(PIECES):
-            nc.tensor.matmul(forget_proj[h][:], forget_w[:], looked_up(h), start=True, stop=True)
-        for h in range(PIECES):
-            nc.tensor.matmul(picked[h][:], identity[:], looked_up(h), start=True, stop=True)
-
-        def of_sentence(products, r):
-            h, s = divmod(r, PER_PIECE)
-            return products[h][:, s * T : (s + 1) * T]
-
-        gate_bias = [held.tile([D, 1], F32, name=f"gate_bias{r}") for r in range(R)]
-        for r in range(R):
-            scaled = scratch.tile([D, T], F32, name="scaled")
-            nc.vector.tensor_scalar(
-                scaled[:], of_sentence(sent_proj, r), HALF_MEAN, half_word_b[:],
-                op0=MULT, op1=ADD, accum_out=gate_bias[r][:],
-            )
+        def looked_up(first_sentence, sentences):
+            first = first_sentence * T // 16
+            return words[:].indirect(offsets[:, first : first + sentences * T // 16])
 
         gate = [held.tile([D, T], F32, name=f"gate{r}") for r in range(R)]
         x = [held.tile([D, T], F32, name=f"x{r}") for r in range(R)]
         x_sum = [held.tile([D, 1], F32, name=f"x_sum{r}") for r in range(R)]
         x_sum_inv = [held.tile([D, 1], F32, name=f"x_sum_inv{r}") for r in range(R)]
         share = [held.tile([D, T], F32, name=f"share{r}") for r in range(R)]
-        f = [held.tile([D, PER_PIECE], F32, name=f"f{h}") for h in range(PIECES)]
-        for h in range(PIECES):
-            a_sum = held.tile([D, PER_PIECE], F32, name=f"a_sum{h}")
-            nc.vector.reduce_sum(a_sum[:], forget_proj[h][:].rearrange("p (r t) -> p r t", t=T), axis=X_AXIS)
-            f_tanh = held.tile([D, PER_PIECE], F32, name=f"f_tanh{h}")
+
+        def make_share(r):
+            nc.scalar.activation(x[r][:], gate[r][:], EXP, scale=0.5, accum_out=x_sum[r][:])
+            nc.vector.reciprocal(x_sum_inv[r][:], x_sum[r][:])
+            nc.vector.tensor_scalar(share[r][:], x[r][:], x_sum_inv[r][:], float(T), op0=MULT, op1=MULT)
+
+        for r in range(R):
+            sent_proj = psum.tile([D, T], F32, name="sent_proj", tag="summed")
+            nc.tensor.matmul(sent_proj[:], sent_w[:], looked_up(r, 1), start=True, stop=True)
+            word_proj = psum.tile([D, T], F32, name="word_proj", tag="word_proj")
+            nc.tensor.matmul(word_proj[:], word_w[:], looked_up(r, 1), start=True, stop=True)
+
+            scaled = scratch.tile([D, T], F32, name="scaled")
+            gate_bias = held.tile([D, 1], F32, name=f"gate_bias{r}")
+            nc.vector.tensor_scalar(
+                scaled[:], sent_proj[:], HALF_MEAN, half_word_b[:],
+                op0=MULT, op1=ADD, accum_out=gate_bias[:],
+            )
+            nc.scalar.activation(gate[r][:], word_proj[:], TANH, bias=gate_bias[:], scale=0.5)
+            if r > 0:
+                make_share(r - 1)
+        make_share(R - 1)
+
+        f = [held.tile([D, PAIR], F32, name=f"f{h}") for h in range(PAIRS)]
+        for h in range(PAIRS):
+            forget_proj = psum.tile([D, PAIR * T], F32, name="forget_proj", tag="summed")
+            nc.tensor.matmul(forget_proj[:], forget_w[:], looked_up(h * PAIR, PAIR), start=True, stop=True)
+            a_sum = held.tile([D, PAIR], F32, name=f"a_sum{h}")
+            nc.vector.reduce_sum(a_sum[:], forget_proj[:].rearrange("p (r t) -> p r t", t=T), axis=X_AXIS)
+            f_tanh = held.tile([D, PAIR], F32, name=f"f_tanh{h}")
             nc.scalar.activation(f_tanh[:], a_sum[:], TANH, bias=half_forget_b[:], scale=HALF_MEAN)
             nc.vector.tensor_scalar(f[h][:], f_tanh[:], 0.5, 0.5, op0=MULT, op1=ADD)
 
-            sentences = range(h * PER_PIECE, (h + 1) * PER_PIECE)
-            for r in sentences:
-                nc.scalar.activation(gate[r][:], of_sentence(word_proj, r), TANH, bias=gate_bias[r][:], scale=0.5)
-            for r in sentences:
-                nc.scalar.activation(x[r][:], gate[r][:], EXP, scale=0.5, accum_out=x_sum[r][:])
-            for r in sentences:
-                nc.vector.reciprocal(x_sum_inv[r][:], x_sum[r][:])
-                nc.vector.tensor_scalar(share[r][:], x[r][:], x_sum_inv[r][:], float(T), op0=MULT, op1=MULT)
-
         result = held.tile([D, N], F32, name="result")
         for r in range(R):
-            h, s = divmod(r, PER_PIECE)
+            h, s = divmod(r, PAIR)
+            picked = psum.tile([D, T], F32, name="picked", tag="picked", bufs=R)
+            nc.tensor.matmul(picked[:], identity[:], looked_up(r, 1), start=True, stop=True)
             nc.vector.scalar_tensor_tensor(
-                result[:, r * T : (r + 1) * T], share[r][:], f[h][:, s : s + 1], of_sentence(picked, r),
+                result[:, r * T : (r + 1) * T], share[r][:], f[h][:, s : s + 1], picked[:],
                 op0=ADD, op1=MULT,
             )
             nc.sync.dma_start(out[:, r * T : (r + 1) * T], result[:, r * T : (r + 1) * T])

@@ -14,6 +14,7 @@ FLOPS = 3 * 2 * D * D * N
 BF16, F32, U16 = mybir.dt.bfloat16, mybir.dt.float32, mybir.dt.uint16
 MULT, ADD = mybir.AluOpType.mult, mybir.AluOpType.add
 TANH, EXP = mybir.ActivationFunctionType.Tanh, mybir.ActivationFunctionType.Exp
+COPY = mybir.ActivationFunctionType.Copy
 X_AXIS = mybir.AxisListType.X
 
 
@@ -91,7 +92,7 @@ def tile_slstm_kernel(tc, table, w_word, w_sent, w_forget, b_word, b_forget, off
             nc.vector.reduce_sum(a_sum[:], forget_proj[:].rearrange("p (r t) -> p r t", t=T), axis=X_AXIS)
             f_tanh = held.tile([D, PAIR], F32, name=f"f_tanh{h}")
             nc.scalar.activation(f_tanh[:], a_sum[:], TANH, bias=half_forget_b[:], scale=HALF_MEAN)
-            nc.vector.tensor_scalar(f[h][:], f_tanh[:], 0.5, 0.5, op0=MULT, op1=ADD)
+            nc.scalar.activation(f[h][:], f_tanh[:], COPY, bias=0.5, scale=0.5)
 
         result = held.tile([D, N], F32, name="result")
         for r in range(R):

import concourse.mybir as mybir
from concourse.masks import make_identity

D = 128
S = 4096
N = 1024
T = 256
R = N // T
PAIR = 2
PAIRS = R // PAIR
HALF_MEAN = 0.5 / T
FLOPS = 3 * 2 * D * D * N

BF16, F32, U16 = mybir.dt.bfloat16, mybir.dt.float32, mybir.dt.uint16
MULT, ADD = mybir.AluOpType.mult, mybir.AluOpType.add
TANH, EXP = mybir.ActivationFunctionType.Tanh, mybir.ActivationFunctionType.Exp
COPY = mybir.ActivationFunctionType.Copy
X_AXIS = mybir.AxisListType.X


def tile_slstm_kernel(tc, table, w_word, w_sent, w_forget, b_word, b_forget, offs, out):
    nc = tc.nc
    with (
        tc.tile_pool(name="held", bufs=1) as held,
        tc.tile_pool(name="scratch", bufs=2) as scratch,
        tc.psum_pool(name="psum", bufs=2) as psum,
    ):
        words = held.tile([D, S], BF16, name="words")
        nc.sync.dma_start(words[:], table)
        offsets = held.tile([D, N // 16], U16, name="offsets")
        nc.sync.dma_start(offsets[:], offs)
        sent_w = held.tile([D, D], BF16, name="sent_w")
        nc.scalar.dma_start(sent_w[:], w_sent)
        word_b = held.tile([D, 1], F32, name="word_b")
        nc.scalar.dma_start(word_b[:], b_word)
        word_w = held.tile([D, D], BF16, name="word_w")
        nc.scalar.dma_start(word_w[:], w_word)
        forget_w = held.tile([D, D], BF16, name="forget_w")
        nc.sync.dma_start(forget_w[:], w_forget)
        forget_b = held.tile([D, 1], F32, name="forget_b")
        nc.sync.dma_start(forget_b[:], b_forget)
        identity = held.tile([D, D], BF16, name="identity")
        make_identity(nc, identity[:])

        primer = held.tile([D, 1], F32, name="primer")
        nc.vector.memset(primer[:], 0.0)
        primed = held.tile([D, 1], F32, name="primed")
        nc.scalar.activation(primed[:], primer[:], TANH)

        half_word_b = held.tile([D, 1], F32, name="half_word_b")
        nc.vector.tensor_scalar(half_word_b[:], word_b[:], 0.5, None, op0=MULT)
        half_forget_b = held.tile([D, 1], F32, name="half_forget_b")
        nc.vector.tensor_scalar(half_forget_b[:], forget_b[:], 0.5, None, op0=MULT)

        def looked_up(first_sentence, sentences):
            first = first_sentence * T // 16
            return words[:].indirect(offsets[:, first : first + sentences * T // 16])

        gate = [held.tile([D, T], F32, name=f"gate{r}") for r in range(R)]
        x = [held.tile([D, T], F32, name=f"x{r}") for r in range(R)]
        x_sum = [held.tile([D, 1], F32, name=f"x_sum{r}") for r in range(R)]
        x_sum_inv = [held.tile([D, 1], F32, name=f"x_sum_inv{r}") for r in range(R)]
        share = [held.tile([D, T], F32, name=f"share{r}") for r in range(R)]

        def make_share(r):
            nc.scalar.activation(x[r][:], gate[r][:], EXP, scale=0.5, accum_out=x_sum[r][:])
            nc.vector.reciprocal(x_sum_inv[r][:], x_sum[r][:])
            nc.vector.tensor_scalar(share[r][:], x[r][:], x_sum_inv[r][:], float(T), op0=MULT, op1=MULT)

        for r in range(R):
            sent_proj = psum.tile([D, T], F32, name="sent_proj", tag="summed")
            nc.tensor.matmul(sent_proj[:], sent_w[:], looked_up(r, 1), start=True, stop=True)
            word_proj = psum.tile([D, T], F32, name="word_proj", tag="word_proj")
            nc.tensor.matmul(word_proj[:], word_w[:], looked_up(r, 1), start=True, stop=True)

            scaled = scratch.tile([D, T], F32, name="scaled")
            gate_bias = held.tile([D, 1], F32, name=f"gate_bias{r}")
            nc.vector.tensor_scalar(
                scaled[:], sent_proj[:], HALF_MEAN, half_word_b[:],
                op0=MULT, op1=ADD, accum_out=gate_bias[:],
            )
            nc.scalar.activation(gate[r][:], word_proj[:], TANH, bias=gate_bias[:], scale=0.5)
            if r > 0:
                make_share(r - 1)
        make_share(R - 1)

        f = [held.tile([D, PAIR], F32, name=f"f{h}") for h in range(PAIRS)]
        for h in range(PAIRS):
            forget_proj = psum.tile([D, PAIR * T], F32, name="forget_proj", tag="summed")
            nc.tensor.matmul(forget_proj[:], forget_w[:], looked_up(h * PAIR, PAIR), start=True, stop=True)
            a_sum = held.tile([D, PAIR], F32, name=f"a_sum{h}")
            nc.vector.reduce_sum(a_sum[:], forget_proj[:].rearrange("p (r t) -> p r t", t=T), axis=X_AXIS)
            f_tanh = held.tile([D, PAIR], F32, name=f"f_tanh{h}")
            nc.scalar.activation(f_tanh[:], a_sum[:], TANH, bias=half_forget_b[:], scale=HALF_MEAN)
            nc.scalar.activation(f[h][:], f_tanh[:], COPY, bias=0.5, scale=0.5)

        result = held.tile([D, N], F32, name="result")
        for r in range(R):
            h, s = divmod(r, PAIR)
            picked = psum.tile([D, T], F32, name="picked", tag="picked", bufs=R)
            nc.tensor.matmul(picked[:], identity[:], looked_up(r, 1), start=True, stop=True)
            nc.vector.scalar_tensor_tensor(
                result[:, r * T : (r + 1) * T], share[r][:], f[h][:, s : s + 1], picked[:],
                op0=ADD, op1=MULT,
            )
            nc.sync.dma_start(out[:, r * T : (r + 1) * T], result[:, r * T : (r + 1) * T])
